import numpy as np
import ml_dtypes


def mxq(x, axis, fmt="e4m3"):
    dtype, down = {"e4m3": (ml_dtypes.float8_e4m3fn, 7), "e5m2": (ml_dtypes.float8_e5m2, 14)}[fmt]
    v = np.moveaxis(np.asarray(x, np.float32).astype(ml_dtypes.bfloat16).astype(np.float64), axis, -1)
    blocks = v.reshape(v.shape[:-1] + (-1, 32))
    amax = np.abs(blocks).max(-1, keepdims=True)
    byte = np.maximum(np.where(amax > 0, np.frexp(amax)[1] - 1 + 127, 0) - down, 1)
    scale = np.exp2(byte - 127.0)
    codes = (blocks / scale).astype(np.float32).astype(dtype).astype(np.float64)
    return np.moveaxis((codes * scale).reshape(v.shape), -1, axis)


WIDE = False


def mx_kscale(k):
    if not WIDE:
        return np.ones(k)
    levels = np.array([10, -10, 5, -5, 0])
    a = np.random.permutation(np.resize(levels, k // 512 * 4)).reshape(k // 512, 4)
    idx = np.arange(k)
    return np.exp2(a[idx // 512, idx % 128 // 32])


BF16 = ml_dtypes.bfloat16


def bf(x):
    return np.asarray(x, np.float32).astype(BF16)


def f64(x):
    return np.asarray(x).astype(np.float64)


E2M1 = np.array([0.0, 0.5, 1.0, 1.5, 2.0, 3.0, 4.0, 6.0, -0.0, -0.5, -1.0, -1.5, -2.0, -3.0, -4.0, -6.0])


def pack_weight(w, fmt):
    k, n = w.shape
    w = f64(bf(w)).reshape(k // 32, 32, n)
    amax = np.abs(w).max(1)
    if fmt == "e4m3":
        byte = np.frexp(amax)[1] - 1 + 127 - 7
    else:
        mant, ex = np.frexp(amax / 6.0)
        byte = np.where(mant > 0.5, ex, ex - 1) + 127
    byte = np.clip(np.where(amax > 0, byte, 1), 1, 254)
    scaled = (w * np.exp2(127.0 - byte)[:, None, :]).reshape(k, n).astype(np.float32)
    by_word = np.ascontiguousarray(scaled.reshape(k // 512, 128, 4, n).transpose(0, 1, 3, 2))
    if fmt == "e4m3":
        words = by_word.astype(ml_dtypes.float8_e4m3fn).view(np.uint8)
    else:
        c = by_word.astype(ml_dtypes.float4_e2m1fn).view(np.uint8) & 0xF
        words = c[..., 0::2] | (c[..., 1::2] << 4)
    return np.ascontiguousarray(words), np.ascontiguousarray(byte.astype(np.uint8).reshape(k // 512, 16, n))


def unpack_weight(words, scales, fmt):
    g, p, n, _ = words.shape
    if fmt == "e4m3":
        vals = np.ascontiguousarray(words).view(ml_dtypes.float8_e4m3fn).astype(np.float64)
    else:
        nib = np.empty((g, p, n, 4), np.uint8)
        nib[..., 0::2] = words & 0xF
        nib[..., 1::2] = words >> 4
        vals = E2M1[nib]
    vals = vals * np.repeat(np.exp2(scales.astype(np.float64) - 127.0), 8, axis=1)[..., None]
    return vals.transpose(0, 1, 3, 2).reshape(g * 512, n)


B, D_IN, D_H = 4096, 512, 512
FMT = "e4m3"


def sigmoid(v):
    return 1.0 / (1.0 + np.exp(-v))


def setup_inputs():
    s, t = mx_kscale(D_IN), mx_kscale(D_H)

    def w_in():
        return pack_weight(np.ascontiguousarray((np.random.standard_normal((D_H, D_IN)) * 0.6 / np.sqrt(D_IN) / s[None, :]).T), FMT)

    def w_rec():
        return pack_weight(np.ascontiguousarray((np.random.standard_normal((D_H, D_H)) * 0.6 / np.sqrt(D_H) / t[None, :]).T), FMT)

    def bias():
        return bf(np.random.standard_normal(D_H) * 0.3)

    incoming = bf(np.random.standard_normal((B, D_IN)) * s)
    h = bf(np.random.standard_normal((B, D_H)) * t)
    W_i_words, W_i_scales = w_in()
    b_W_i = bias()
    W_c_words, W_c_scales = w_in()
    b_W_c = bias()
    U_i_words, U_i_scales = w_rec()
    b_U_i = bias()
    U_c_words, U_c_scales = w_rec()
    b_U_c = bias()
    return {"incoming": incoming, "h": h,
            "W_i_words": W_i_words, "W_i_scales": W_i_scales, "b_W_i": b_W_i,
            "W_c_words": W_c_words, "W_c_scales": W_c_scales, "b_W_c": b_W_c,
            "U_i_words": U_i_words, "U_i_scales": U_i_scales, "b_U_i": b_U_i,
            "U_c_words": U_c_words, "U_c_scales": U_c_scales, "b_U_c": b_U_c}


def reference(incoming, h, W_i_words, W_i_scales, b_W_i, W_c_words, W_c_scales, b_W_c, U_i_words, U_i_scales, b_U_i, U_c_words, U_c_scales, b_U_c):
    xq = mxq(f64(incoming), 1, "e4m3")
    hq = mxq(f64(h), 1, "e4m3")
    I = sigmoid((xq @ unpack_weight(W_i_words, W_i_scales, FMT)) + f64(b_W_i) + (hq @ unpack_weight(U_i_words, U_i_scales, FMT)) + f64(b_U_i))
    C_head = (xq @ unpack_weight(W_c_words, W_c_scales, FMT)) + f64(b_W_c) + (hq @ unpack_weight(U_c_words, U_c_scales, FMT)) + f64(b_U_c)
    return I * C_head

@@ -1,0 +1,172 @@
+from contextlib import ExitStack
+
+import concourse.mybir as mybir
+from concourse.masks import make_identity
+
+F32 = mybir.dt.float32
+BF16 = mybir.dt.bfloat16
+I32 = mybir.dt.int32
+U32 = mybir.dt.uint32
+U8 = mybir.dt.uint8
+FP8X4 = mybir.dt.float8_e4m3fn_x4
+ADD = mybir.AluOpType.add
+MULT = mybir.AluOpType.mult
+SIGMOID = mybir.ActivationFunctionType.Sigmoid
+
+P = 128
+PACK = 4
+BATCH = 4096
+K = P * PACK
+UNITS = 512
+TILES = BATCH // P
+ROUND = 4
+ROUNDS = TILES // ROUND
+LEAD = 5
+PAIR = 2
+WORDS = K // 2
+
+FLOPS = 4 * 2 * BATCH * K * UNITS
+
+
+def tile_lstmcell_pa_t_kernel(
+    tc,
+    incoming,
+    h,
+    W_i_words,
+    W_i_scales,
+    b_W_i,
+    W_c_words,
+    W_c_scales,
+    b_W_c,
+    U_i_words,
+    U_i_scales,
+    b_U_i,
+    U_c_words,
+    U_c_scales,
+    b_U_c,
+    out,
+):
+    nc = tc.nc
+    operand_rows = [a.rearrange("(p t) k -> p t k", t=TILES) for a in (incoming, h)]
+    out_rows = out.rearrange("(p t) n -> p t n", t=TILES)
+    weights = [(W_i_words, W_i_scales), (U_i_words, U_i_scales), (W_c_words, W_c_scales), (U_c_words, U_c_scales)]
+    biases = [(b_W_i, b_U_i), (b_W_c, b_U_c)]
+
+    with ExitStack() as ctx:
+        ctx.enter_context(tc.manual_schedule())
+        const = ctx.enter_context(tc.tile_pool(name="const", bufs=1))
+        stage = ctx.enter_context(tc.tile_pool(name="stage", bufs=3))
+        gates = ctx.enter_context(tc.tile_pool(name="gates", bufs=4))
+        psum_t = ctx.enter_context(tc.psum_pool(name="psum_t", bufs=4))
+        psum_mx = ctx.enter_context(tc.psum_pool(name="psum_mx", bufs=4))
+
+        ident = const.tile([P, P], F32)
+        make_identity(nc, ident[:])
+        ones = const.tile([P, P], BF16)
+        nc.vector.memset(ones[:], 1.0)
+        bias_rows = const.tile([P, 2, UNITS], BF16)
+        nc.vector.memset(bias_rows[:], 0.0)
+        warm = const.tile([P, 1], F32)
+        nc.vector.memset(warm[:], 0.0)
+
+        for gate in range(2):
+            for row in range(2):
+                nc.scalar.dma_start(out=bias_rows[row : row + 1, gate, :], in_=biases[gate][row].unsqueeze(0))
+        nc.scalar.activation(out=warm[:], in_=warm[:], func=SIGMOID)
+
+        acts = [[None, None] for r in range(ROUNDS)]
+
+        def load_round(r):
+            for o in range(2):
+                rows = const.tile([P, ROUND, K], BF16, name="acts_%d_%d" % (r, o))
+                nc.sync.dma_start(out=rows[:], in_=operand_rows[o][:, r * ROUND : (r + 1) * ROUND, :])
+                acts[r][o] = rows
+
+        for r in range(LEAD):
+            load_round(r)
+        w_codes = const.tile([P, 4, PACK * UNITS], U8, align_bytes=64)
+        for w in range(4):
+            nc.sync.dma_start(
+                out=w_codes[:, w, :].bitcast(I32),
+                in_=weights[w][0].rearrange("g p n t -> (g p) (n t)").bitcast(I32),
+            )
+        for r in range(LEAD, ROUNDS):
+            load_round(r)
+        w_planes = const.tile([P, 4, UNITS], U8, align_bytes=64)
+        nc.vector.memset(w_planes[:].rearrange("p w n -> p (w n)").bitcast(I32), 0)
+        for w in range(4):
+            scale_rows = weights[w][1].rearrange("g (a r) n -> r (g a) n", r=4)
+            for r in range(4):
+                nc.gpsimd.dma_start(out=w_planes[r:P:32, w, :].bitcast(F32), in_=scale_rows[r].bitcast(F32))
+
+        grouped_of = [None] * ROUNDS
+        codes_of = [None] * ROUNDS
+        planes_of = [None] * ROUNDS
+        bias = const.tile([P, 2, UNITS], F32)
+
+        def transpose_round(r):
+            grouped = stage.tile([P, 2 * ROUND * P * PACK], BF16, align_bytes=64)
+            grouped_words = grouped[:].bitcast(F32).rearrange("p (c j b u) -> p c j b u", j=PAIR, b=P, u=2)
+            for o in range(2):
+                for pair in range(ROUND // PAIR):
+                    bank = psum_t.tile([P, PAIR, 2, P], F32)
+                    for j in range(PAIR):
+                        row_words = acts[r][o][:, pair * PAIR + j, :].bitcast(F32)
+                        for u in range(2):
+                            nc.tensor.transpose(bank[:, j, u, :], row_words[:, u:WORDS:2], ident[:])
+                    nc.scalar.copy(
+                        out=grouped_words[:, o * (ROUND // PAIR) + pair],
+                        in_=bank[:].rearrange("p j u b -> p j b u"),
+                    )
+            grouped_of[r] = grouped
+
+        def quantise_round(r):
+            codes = const.tile([P, 2 * ROUND * P], U32, name="codes_%d" % r, align_bytes=64)
+            planes = const.tile([P, 2 * ROUND * P], U8, name="planes_%d" % r, align_bytes=64)
+            nc.vector.quantize_mx(out=codes[:].bitcast(FP8X4), scales=planes[:], in_=grouped_of[r][:])
+            codes_of[r] = codes
+            planes_of[r] = planes
+
+        def spread_biases():
+            for gate in range(2):
+                acc = psum_mx.tile([P, UNITS], F32)
+                nc.tensor.matmul(out=acc[:], lhsT=ones[:], rhs=bias_rows[:, gate, :], start=True, stop=True)
+                nc.vector.tensor_copy(out=bias[:, gate, :], in_=acc[:])
+
+        def gate_sum(r, j, gate):
+            acc = psum_mx.tile([P, UNITS], F32)
+            for o in range(2):
+                cols = slice((o * ROUND + j) * P, (o * ROUND + j + 1) * P)
+                nc.tensor.matmul_mx(
+                    out=acc[:],
+                    lhsT=codes_of[r][:, cols].bitcast(FP8X4),
+                    lhsT_scale=planes_of[r][:, cols],
+                    rhs=w_codes[:, 2 * gate + o, :].bitcast(FP8X4),
+                    rhs_scale=w_planes[:, 2 * gate + o, :],
+                    start=(o == 0),
+                    stop=(o == 1),
+                )
+            return acc
+
+        def multiply_round(r):
+            for j in range(ROUND):
+                acc_i = gate_sum(r, j, 0)
+                gate_i = gates.tile([P, UNITS], F32)
+                nc.vector.tensor_tensor(out=gate_i[:], in0=acc_i[:], in1=bias[:, 0, :], op=ADD)
+                nc.scalar.activation(out=gate_i[:], in_=gate_i[:], func=SIGMOID)
+                acc_c = gate_sum(r, j, 1)
+                c_head = gates.tile([P, UNITS], F32)
+                nc.vector.tensor_tensor(out=c_head[:], in0=acc_c[:], in1=bias[:, 1, :], op=ADD)
+                result = gates.tile([P, UNITS], F32)
+                nc.gpsimd.tensor_tensor(out=result[:], in0=gate_i[:], in1=c_head[:], op=MULT)
+                nc.sync.dma_start(out=out_rows[:, r * ROUND + j, :], in_=result[:])
+
+        for step in range(ROUNDS + LEAD):
+            if step < ROUNDS:
+                transpose_round(step)
+            if 1 <= step <= ROUNDS:
+                quantise_round(step - 1)
+            if step == LEAD:
+                spread_biases()
+            if step >= LEAD:
+                multiply_round(step - LEAD)

@@ -21,7 +21,7 @@ UNITS = 512
 TILES = BATCH // P
 ROUND = 4
 ROUNDS = TILES // ROUND
-LEAD = 5
+LEAD = 3
 PAIR = 2
 WORDS = K // 2
 
@@ -74,30 +74,41 @@ def tile_lstmcell_pa_t_kernel(
                 nc.scalar.dma_start(out=bias_rows[row : row + 1, gate, :], in_=biases[gate][row].unsqueeze(0))
         nc.scalar.activation(out=warm[:], in_=warm[:], func=SIGMOID)
 
-        acts = [[None, None] for r in range(ROUNDS)]
-
-        def load_round(r):
-            for o in range(2):
-                rows = const.tile([P, ROUND, K], BF16, name="acts_%d_%d" % (r, o))
-                nc.sync.dma_start(out=rows[:], in_=operand_rows[o][:, r * ROUND : (r + 1) * ROUND, :])
-                acts[r][o] = rows
-
-        for r in range(LEAD):
-            load_round(r)
+        w_planes = const.tile([P, 4, UNITS], U8, align_bytes=64)
+        nc.vector.memset(w_planes[:].rearrange("p w n -> p (w n)").bitcast(I32), 0)
         w_codes = const.tile([P, 4, PACK * UNITS], U8, align_bytes=64)
-        for w in range(4):
+        acts = [
+            [const.tile([P, ROUND, K], BF16, name="acts_%d_%d" % (r, o)) for o in range(2)] for r in range(ROUNDS)
+        ]
+
+        def load_acts(r, o):
+            nc.sync.dma_start(out=acts[r][o][:], in_=operand_rows[o][:, r * ROUND : (r + 1) * ROUND, :])
+
+        def load_codes(w):
             nc.sync.dma_start(
                 out=w_codes[:, w, :].bitcast(I32),
                 in_=weights[w][0].rearrange("g p n t -> (g p) (n t)").bitcast(I32),
             )
-        for r in range(LEAD, ROUNDS):
-            load_round(r)
-        w_planes = const.tile([P, 4, UNITS], U8, align_bytes=64)
-        nc.vector.memset(w_planes[:].rearrange("p w n -> p (w n)").bitcast(I32), 0)
-        for w in range(4):
+
+        def load_scale_rows(w, r):
             scale_rows = weights[w][1].rearrange("g (a r) n -> r (g a) n", r=4)
-            for r in range(4):
-                nc.gpsimd.dma_start(out=w_planes[r:P:32, w, :].bitcast(F32), in_=scale_rows[r].bitcast(F32))
+            nc.sync.dma_start(out=w_planes[r:P:32, w, :].bitcast(I32), in_=scale_rows[r].bitcast(I32))
+
+        load_acts(0, 0)
+        load_acts(0, 1)
+        for r in range(1, LEAD):
+            for o in range(2):
+                load_acts(r, o)
+                w = 2 * (r - 1) + o
+                load_scale_rows(w, 0)
+                load_scale_rows(w, 1)
+        for w in range(4):
+            load_codes(w)
+            load_scale_rows(w, 2)
+            load_scale_rows(w, 3)
+        for r in range(LEAD, ROUNDS):
+            for o in range(2):
+                load_acts(r, o)
 
         grouped_of = [None] * ROUNDS
         codes_of = [None] * ROUNDS

@@ -21,7 +21,9 @@ UNITS = 512
 TILES = BATCH // P
 ROUND = 4
 ROUNDS = TILES // ROUND
-LEAD = 3
+LEAD = 2
+T_BANKS = 4
+VECTOR_PRODUCTS = 2
 PAIR = 2
 WORDS = K // 2
 
@@ -57,8 +59,8 @@ def tile_lstmcell_pa_t_kernel(
         const = ctx.enter_context(tc.tile_pool(name="const", bufs=1))
         stage = ctx.enter_context(tc.tile_pool(name="stage", bufs=3))
         gates = ctx.enter_context(tc.tile_pool(name="gates", bufs=4))
-        psum_t = ctx.enter_context(tc.psum_pool(name="psum_t", bufs=4))
-        psum_mx = ctx.enter_context(tc.psum_pool(name="psum_mx", bufs=4))
+        psum_t = ctx.enter_context(tc.psum_pool(name="psum_t", bufs=T_BANKS))
+        psum_mx = ctx.enter_context(tc.psum_pool(name="psum_mx", bufs=8 - T_BANKS))
 
         ident = const.tile([P, P], F32)
         make_identity(nc, ident[:])
@@ -94,18 +96,12 @@ def tile_lstmcell_pa_t_kernel(
             scale_rows = weights[w][1].rearrange("g (a r) n -> r (g a) n", r=4)
             nc.sync.dma_start(out=w_planes[r:P:32, w, :].bitcast(I32), in_=scale_rows[r].bitcast(I32))
 
-        load_acts(0, 0)
-        load_acts(0, 1)
-        for r in range(1, LEAD):
-            for o in range(2):
-                load_acts(r, o)
-                w = 2 * (r - 1) + o
-                load_scale_rows(w, 0)
-                load_scale_rows(w, 1)
-        for w in range(4):
-            load_codes(w)
-            load_scale_rows(w, 2)
-            load_scale_rows(w, 3)
+        first_loads = [(load_acts, r, o) for r in range(LEAD) for o in range(2)]
+        first_loads += [(load_codes, w) for w in range(4)]
+        for n, (load, *which) in enumerate(first_loads):
+            load(*which)
+            for s in range(2 * n, 2 * n + 2):
+                load_scale_rows(s // 4, s % 4)
         for r in range(LEAD, ROUNDS):
             for o in range(2):
                 load_acts(r, o)
@@ -169,7 +165,8 @@ def tile_lstmcell_pa_t_kernel(
                 c_head = gates.tile([P, UNITS], F32)
                 nc.vector.tensor_tensor(out=c_head[:], in0=acc_c[:], in1=bias[:, 1, :], op=ADD)
                 result = gates.tile([P, UNITS], F32)
-                nc.gpsimd.tensor_tensor(out=result[:], in0=gate_i[:], in1=c_head[:], op=MULT)
+                engine = nc.vector if r * ROUND + j >= TILES - VECTOR_PRODUCTS else nc.gpsimd
+                engine.tensor_tensor(out=result[:], in0=gate_i[:], in1=c_head[:], op=MULT)
                 nc.sync.dma_start(out=out_rows[:, r * ROUND + j, :], in_=result[:])
 
         for step in range(ROUNDS + LEAD):

@@ -21,11 +21,9 @@ UNITS = 512
 TILES = BATCH // P
 ROUND = 4
 ROUNDS = TILES // ROUND
-LEAD = 2
-T_BANKS = 4
-VECTOR_PRODUCTS = 2
 PAIR = 2
-WORDS = K // 2
+GROUP = 2
+BANKS = 8
 
 FLOPS = 4 * 2 * BATCH * K * UNITS
 
@@ -59,8 +57,6 @@ def tile_lstmcell_pa_t_kernel(
         const = ctx.enter_context(tc.tile_pool(name="const", bufs=1))
         stage = ctx.enter_context(tc.tile_pool(name="stage", bufs=3))
         gates = ctx.enter_context(tc.tile_pool(name="gates", bufs=4))
-        psum_t = ctx.enter_context(tc.psum_pool(name="psum_t", bufs=T_BANKS))
-        psum_mx = ctx.enter_context(tc.psum_pool(name="psum_mx", bufs=8 - T_BANKS))
 
         ident = const.tile([P, P], F32)
         make_identity(nc, ident[:])
@@ -70,111 +66,88 @@ def tile_lstmcell_pa_t_kernel(
         nc.vector.memset(bias_rows[:], 0.0)
         warm = const.tile([P, 1], F32)
         nc.vector.memset(warm[:], 0.0)
+        w_planes = const.tile([P, 4, UNITS], U8, align_bytes=64)
+        nc.vector.memset(w_planes[:].rearrange("p w n -> p (w n)").bitcast(I32), 0)
 
         for gate in range(2):
             for row in range(2):
                 nc.scalar.dma_start(out=bias_rows[row : row + 1, gate, :], in_=biases[gate][row].unsqueeze(0))
         nc.scalar.activation(out=warm[:], in_=warm[:], func=SIGMOID)
 
-        w_planes = const.tile([P, 4, UNITS], U8, align_bytes=64)
-        nc.vector.memset(w_planes[:].rearrange("p w n -> p (w n)").bitcast(I32), 0)
-        w_codes = const.tile([P, 4, PACK * UNITS], U8, align_bytes=64)
         acts = [
             [const.tile([P, ROUND, K], BF16, name="acts_%d_%d" % (r, o)) for o in range(2)] for r in range(ROUNDS)
         ]
-
-        def load_acts(r, o):
-            nc.sync.dma_start(out=acts[r][o][:], in_=operand_rows[o][:, r * ROUND : (r + 1) * ROUND, :])
-
-        def load_codes(w):
+        for r in range(ROUNDS):
+            for o in range(2):
+                nc.sync.dma_start(out=acts[r][o][:], in_=operand_rows[o][:, r * ROUND : (r + 1) * ROUND, :])
+        w_codes = const.tile([P, 4, PACK * UNITS], U8, align_bytes=64)
+        for w in range(4):
             nc.sync.dma_start(
                 out=w_codes[:, w, :].bitcast(I32),
                 in_=weights[w][0].rearrange("g p n t -> (g p) (n t)").bitcast(I32),
             )
-
-        def load_scale_rows(w, r):
+        for w in range(4):
             scale_rows = weights[w][1].rearrange("g (a r) n -> r (g a) n", r=4)
-            nc.sync.dma_start(out=w_planes[r:P:32, w, :].bitcast(I32), in_=scale_rows[r].bitcast(I32))
+            for r in range(4):
+                nc.gpsimd.dma_start(out=w_planes[r:P:32, w, :].bitcast(F32), in_=scale_rows[r].bitcast(F32))
 
-        first_loads = [(load_acts, r, o) for r in range(LEAD) for o in range(2)]
-        first_loads += [(load_codes, w) for w in range(4)]
-        for n, (load, *which) in enumerate(first_loads):
-            load(*which)
-            for s in range(2 * n, 2 * n + 2):
-                load_scale_rows(s // 4, s % 4)
-        for r in range(LEAD, ROUNDS):
-            for o in range(2):
-                load_acts(r, o)
-
+        codes = [const.tile([P, 2 * ROUND * P], U32, name="codes_%d" % r, align_bytes=64) for r in range(ROUNDS)]
+        planes = [const.tile([P, 2 * ROUND * P], U8, name="planes_%d" % r, align_bytes=64) for r in range(ROUNDS)]
         grouped_of = [None] * ROUNDS
-        codes_of = [None] * ROUNDS
-        planes_of = [None] * ROUNDS
-        bias = const.tile([P, 2, UNITS], F32)
-
-        def transpose_round(r):
-            grouped = stage.tile([P, 2 * ROUND * P * PACK], BF16, align_bytes=64)
-            grouped_words = grouped[:].bitcast(F32).rearrange("p (c j b u) -> p c j b u", j=PAIR, b=P, u=2)
-            for o in range(2):
-                for pair in range(ROUND // PAIR):
-                    bank = psum_t.tile([P, PAIR, 2, P], F32)
-                    for j in range(PAIR):
-                        row_words = acts[r][o][:, pair * PAIR + j, :].bitcast(F32)
-                        for u in range(2):
-                            nc.tensor.transpose(bank[:, j, u, :], row_words[:, u:WORDS:2], ident[:])
-                    nc.scalar.copy(
-                        out=grouped_words[:, o * (ROUND // PAIR) + pair],
-                        in_=bank[:].rearrange("p j u b -> p j b u"),
-                    )
-            grouped_of[r] = grouped
 
         def quantise_round(r):
-            codes = const.tile([P, 2 * ROUND * P], U32, name="codes_%d" % r, align_bytes=64)
-            planes = const.tile([P, 2 * ROUND * P], U8, name="planes_%d" % r, align_bytes=64)
-            nc.vector.quantize_mx(out=codes[:].bitcast(FP8X4), scales=planes[:], in_=grouped_of[r][:])
-            codes_of[r] = codes
-            planes_of[r] = planes
+            nc.vector.quantize_mx(out=codes[r][:].bitcast(FP8X4), scales=planes[r][:], in_=grouped_of[r][:])
 
-        def spread_biases():
+        with tc.psum_pool(name="psum_t", bufs=BANKS) as psum_t:
+            for r in range(ROUNDS):
+                grouped = stage.tile([P, 2 * ROUND * P * PACK], BF16, align_bytes=64)
+                grouped_words = grouped[:].bitcast(F32).rearrange("p (c j b u) -> p c j b u", j=PAIR, b=P, u=2)
+                for o in range(2):
+                    row_words = acts[r][o][:].bitcast(F32).rearrange("p j (w u) -> p j u w", u=2)
+                    for pair in range(ROUND // PAIR):
+                        bank = psum_t.tile([P, PAIR, 2, P], F32)
+                        for j in range(PAIR):
+                            for u in range(2):
+                                nc.tensor.transpose(bank[:, j, u, :], row_words[:, pair * PAIR + j, u, :], ident[:])
+                        nc.scalar.copy(
+                            out=grouped_words[:, o * (ROUND // PAIR) + pair],
+                            in_=bank[:].rearrange("p j u b -> p j b u"),
+                        )
+                grouped_of[r] = grouped
+                if r > 0:
+                    quantise_round(r - 1)
+            quantise_round(ROUNDS - 1)
+
+        with tc.psum_pool(name="psum_mx", bufs=BANKS, reuse_waits="tile") as psum_mx:
+            bias = const.tile([P, 2, UNITS], F32)
             for gate in range(2):
                 acc = psum_mx.tile([P, UNITS], F32)
                 nc.tensor.matmul(out=acc[:], lhsT=ones[:], rhs=bias_rows[:, gate, :], start=True, stop=True)
                 nc.vector.tensor_copy(out=bias[:, gate, :], in_=acc[:])
 
-        def gate_sum(r, j, gate):
-            acc = psum_mx.tile([P, UNITS], F32)
-            for o in range(2):
-                cols = slice((o * ROUND + j) * P, (o * ROUND + j + 1) * P)
-                nc.tensor.matmul_mx(
-                    out=acc[:],
-                    lhsT=codes_of[r][:, cols].bitcast(FP8X4),
-                    lhsT_scale=planes_of[r][:, cols],
-                    rhs=w_codes[:, 2 * gate + o, :].bitcast(FP8X4),
-                    rhs_scale=w_planes[:, 2 * gate + o, :],
-                    start=(o == 0),
-                    stop=(o == 1),
-                )
-            return acc
+            def biased_sum(t, gate, dest):
+                r, j = divmod(t, ROUND)
+                acc = psum_mx.tile([P, UNITS], F32)
+                for o in range(2):
+                    cols = slice((o * ROUND + j) * P, (o * ROUND + j + 1) * P)
+                    nc.tensor.matmul_mx(
+                        out=acc[:],
+                        lhsT=codes[r][:, cols].bitcast(FP8X4),
+                        lhsT_scale=planes[r][:, cols],
+                        rhs=w_codes[:, 2 * gate + o, :].bitcast(FP8X4),
+                        rhs_scale=w_planes[:, 2 * gate + o, :],
+                        start=(o == 0),
+                        stop=(o == 1),
+                    )
+                nc.vector.tensor_tensor(out=dest, in0=acc[:], in1=bias[:, gate, :], op=ADD)
 
-        def multiply_round(r):
-            for j in range(ROUND):
-                acc_i = gate_sum(r, j, 0)
-                gate_i = gates.tile([P, UNITS], F32)
-                nc.vector.tensor_tensor(out=gate_i[:], in0=acc_i[:], in1=bias[:, 0, :], op=ADD)
-                nc.scalar.activation(out=gate_i[:], in_=gate_i[:], func=SIGMOID)
-                acc_c = gate_sum(r, j, 1)
-                c_head = gates.tile([P, UNITS], F32)
-                nc.vector.tensor_tensor(out=c_head[:], in0=acc_c[:], in1=bias[:, 1, :], op=ADD)
-                result = gates.tile([P, UNITS], F32)
-                engine = nc.vector if r * ROUND + j >= TILES - VECTOR_PRODUCTS else nc.gpsimd
-                engine.tensor_tensor(out=result[:], in0=gate_i[:], in1=c_head[:], op=MULT)
-                nc.sync.dma_start(out=out_rows[:, r * ROUND + j, :], in_=result[:])
-
-        for step in range(ROUNDS + LEAD):
-            if step < ROUNDS:
-                transpose_round(step)
-            if 1 <= step <= ROUNDS:
-                quantise_round(step - 1)
-            if step == LEAD:
-                spread_biases()
-            if step >= LEAD:
-                multiply_round(step - LEAD)
+            for first in range(0, TILES, GROUP):
+                gate_i = gates.tile([P, GROUP, UNITS], F32)
+                c_head = gates.tile([P, GROUP, UNITS], F32)
+                result = gates.tile([P, GROUP, UNITS], F32)
+                for g in range(GROUP):
+                    biased_sum(first + g, 0, gate_i[:, g, :])
+                    nc.scalar.activation(out=gate_i[:, g, :], in_=gate_i[:, g, :], func=SIGMOID)
+                    biased_sum(first + g, 1, c_head[:, g, :])
+                nc.gpsimd.tensor_tensor(out=result[:], in0=gate_i[:], in1=c_head[:], op=MULT)
+                nc.sync.dma_start(out=out_rows[:, first : first + GROUP, :], in_=result[:])

@@ -23,6 +23,7 @@ ROUND = 4
 ROUNDS = TILES // ROUND
 PAIR = 2
 GROUP = 2
+VECTOR_GROUPS = 2
 BANKS = 8
 
 FLOPS = 4 * 2 * BATCH * K * UNITS
@@ -141,13 +142,22 @@ def tile_lstmcell_pa_t_kernel(
                     )
                 nc.vector.tensor_tensor(out=dest, in0=acc[:], in1=bias[:, gate, :], op=ADD)
 
+            def product(engine, first, gate_i, c_head):
+                result = gates.tile([P, GROUP, UNITS], F32)
+                engine.tensor_tensor(out=result[:], in0=gate_i[:], in1=c_head[:], op=MULT)
+                nc.sync.dma_start(out=out_rows[:, first : first + GROUP, :], in_=result[:])
+
+            left_to_vector = []
             for first in range(0, TILES, GROUP):
                 gate_i = gates.tile([P, GROUP, UNITS], F32)
                 c_head = gates.tile([P, GROUP, UNITS], F32)
-                result = gates.tile([P, GROUP, UNITS], F32)
                 for g in range(GROUP):
                     biased_sum(first + g, 0, gate_i[:, g, :])
                     nc.scalar.activation(out=gate_i[:, g, :], in_=gate_i[:, g, :], func=SIGMOID)
                     biased_sum(first + g, 1, c_head[:, g, :])
-                nc.gpsimd.tensor_tensor(out=result[:], in0=gate_i[:], in1=c_head[:], op=MULT)
-                nc.sync.dma_start(out=out_rows[:, first : first + GROUP, :], in_=result[:])
+                if first < TILES - VECTOR_GROUPS * GROUP:
+                    product(nc.gpsimd, first, gate_i, c_head)
+                else:
+                    left_to_vector.append((first, gate_i, c_head))
+            for first, gate_i, c_head in left_to_vector:
+                product(nc.vector, first, gate_i, c_head)

@@ -22,9 +22,10 @@ TILES = BATCH // P
 ROUND = 4
 ROUNDS = TILES // ROUND
 PAIR = 2
-GROUP = 2
-VECTOR_GROUPS = 2
-BANKS = 8
+T_BANKS = 4
+MX_BANKS = 4
+QUANTISE_AFTER = 1
+VECTOR_TILES = 2
 
 FLOPS = 4 * 2 * BATCH * K * UNITS
 
@@ -56,9 +57,13 @@ def tile_lstmcell_pa_t_kernel(
     with ExitStack() as ctx:
         ctx.enter_context(tc.manual_schedule())
         const = ctx.enter_context(tc.tile_pool(name="const", bufs=1))
-        stage = ctx.enter_context(tc.tile_pool(name="stage", bufs=3))
-        gates = ctx.enter_context(tc.tile_pool(name="gates", bufs=4))
+        stage = ctx.enter_context(tc.tile_pool(name="stage", bufs=2))
+        gates = ctx.enter_context(tc.tile_pool(name="gates", bufs=6))
+        psum_t = ctx.enter_context(tc.psum_pool(name="psum_t", bufs=T_BANKS))
+        psum_mx = ctx.enter_context(tc.psum_pool(name="psum_mx", bufs=MX_BANKS))
 
+        w_planes = const.tile([P, 4, UNITS], U8, align_bytes=64)
+        nc.vector.memset(w_planes[:].rearrange("p w n -> p (w n)").bitcast(I32), 0)
         ident = const.tile([P, P], F32)
         make_identity(nc, ident[:])
         ones = const.tile([P, P], BF16)
@@ -67,8 +72,6 @@ def tile_lstmcell_pa_t_kernel(
         nc.vector.memset(bias_rows[:], 0.0)
         warm = const.tile([P, 1], F32)
         nc.vector.memset(warm[:], 0.0)
-        w_planes = const.tile([P, 4, UNITS], U8, align_bytes=64)
-        nc.vector.memset(w_planes[:].rearrange("p w n -> p (w n)").bitcast(I32), 0)
 
         for gate in range(2):
             for row in range(2):
@@ -78,86 +81,94 @@ def tile_lstmcell_pa_t_kernel(
         acts = [
             [const.tile([P, ROUND, K], BF16, name="acts_%d_%d" % (r, o)) for o in range(2)] for r in range(ROUNDS)
         ]
-        for r in range(ROUNDS):
+
+        def load_round(r):
             for o in range(2):
                 nc.sync.dma_start(out=acts[r][o][:], in_=operand_rows[o][:, r * ROUND : (r + 1) * ROUND, :])
+
+        load_round(0)
+        for w in range(4):
+            scale_rows = weights[w][1].rearrange("g (a r) n -> r (g a) n", r=4)
+            for r in range(4):
+                nc.sync.dma_start(out=w_planes[r:P:32, w, :].bitcast(I32), in_=scale_rows[r].bitcast(I32))
         w_codes = const.tile([P, 4, PACK * UNITS], U8, align_bytes=64)
         for w in range(4):
             nc.sync.dma_start(
                 out=w_codes[:, w, :].bitcast(I32),
                 in_=weights[w][0].rearrange("g p n t -> (g p) (n t)").bitcast(I32),
             )
-        for w in range(4):
-            scale_rows = weights[w][1].rearrange("g (a r) n -> r (g a) n", r=4)
-            for r in range(4):
-                nc.gpsimd.dma_start(out=w_planes[r:P:32, w, :].bitcast(F32), in_=scale_rows[r].bitcast(F32))
+        for r in range(1, ROUNDS):
+            load_round(r)
 
         codes = [const.tile([P, 2 * ROUND * P], U32, name="codes_%d" % r, align_bytes=64) for r in range(ROUNDS)]
         planes = [const.tile([P, 2 * ROUND * P], U8, name="planes_%d" % r, align_bytes=64) for r in range(ROUNDS)]
         grouped_of = [None] * ROUNDS
 
+        def transpose_round(r):
+            grouped = stage.tile([P, 2 * ROUND * P * PACK], BF16, align_bytes=64)
+            grouped_words = grouped[:].bitcast(F32).rearrange("p (c j b u) -> p c j b u", j=PAIR, b=P, u=2)
+            for o in range(2):
+                row_words = acts[r][o][:].bitcast(F32).rearrange("p j (w u) -> p j u w", u=2)
+                for pair in range(ROUND // PAIR):
+                    bank = psum_t.tile([P, PAIR, 2, P], F32)
+                    for j in range(PAIR):
+                        for u in range(2):
+                            nc.tensor.transpose(bank[:, j, u, :], row_words[:, pair * PAIR + j, u, :], ident[:])
+                    nc.scalar.copy(
+                        out=grouped_words[:, o * (ROUND // PAIR) + pair],
+                        in_=bank[:].rearrange("p j u b -> p j b u"),
+                    )
+            grouped_of[r] = grouped
+
         def quantise_round(r):
             nc.vector.quantize_mx(out=codes[r][:].bitcast(FP8X4), scales=planes[r][:], in_=grouped_of[r][:])
 
-        with tc.psum_pool(name="psum_t", bufs=BANKS) as psum_t:
-            for r in range(ROUNDS):
-                grouped = stage.tile([P, 2 * ROUND * P * PACK], BF16, align_bytes=64)
-                grouped_words = grouped[:].bitcast(F32).rearrange("p (c j b u) -> p c j b u", j=PAIR, b=P, u=2)
-                for o in range(2):
-                    row_words = acts[r][o][:].bitcast(F32).rearrange("p j (w u) -> p j u w", u=2)
-                    for pair in range(ROUND // PAIR):
-                        bank = psum_t.tile([P, PAIR, 2, P], F32)
-                        for j in range(PAIR):
-                            for u in range(2):
-                                nc.tensor.transpose(bank[:, j, u, :], row_words[:, pair * PAIR + j, u, :], ident[:])
-                        nc.scalar.copy(
-                            out=grouped_words[:, o * (ROUND // PAIR) + pair],
-                            in_=bank[:].rearrange("p j u b -> p j b u"),
-                        )
-                grouped_of[r] = grouped
-                if r > 0:
-                    quantise_round(r - 1)
-            quantise_round(ROUNDS - 1)
+        bias = const.tile([P, 2, UNITS], F32)
 
-        with tc.psum_pool(name="psum_mx", bufs=BANKS, reuse_waits="tile") as psum_mx:
-            bias = const.tile([P, 2, UNITS], F32)
-            for gate in range(2):
-                acc = psum_mx.tile([P, UNITS], F32)
-                nc.tensor.matmul(out=acc[:], lhsT=ones[:], rhs=bias_rows[:, gate, :], start=True, stop=True)
-                nc.vector.tensor_copy(out=bias[:, gate, :], in_=acc[:])
+        def biased_sum(t, gate, dest):
+            r, j = divmod(t, ROUND)
+            acc = psum_mx.tile([P, UNITS], F32)
+            for o in range(2):
+                cols = slice((o * ROUND + j) * P, (o * ROUND + j + 1) * P)
+                nc.tensor.matmul_mx(
+                    out=acc[:],
+                    lhsT=codes[r][:, cols].bitcast(FP8X4),
+                    lhsT_scale=planes[r][:, cols],
+                    rhs=w_codes[:, 2 * gate + o, :].bitcast(FP8X4),
+                    rhs_scale=w_planes[:, 2 * gate + o, :],
+                    start=(o == 0),
+                    stop=(o == 1),
+                )
+            nc.vector.tensor_tensor(out=dest, in0=acc[:], in1=bias[:, gate, :], op=ADD)
 
-            def biased_sum(t, gate, dest):
-                r, j = divmod(t, ROUND)
-                acc = psum_mx.tile([P, UNITS], F32)
-                for o in range(2):
-                    cols = slice((o * ROUND + j) * P, (o * ROUND + j + 1) * P)
-                    nc.tensor.matmul_mx(
-                        out=acc[:],
-                        lhsT=codes[r][:, cols].bitcast(FP8X4),
-                        lhsT_scale=planes[r][:, cols],
-                        rhs=w_codes[:, 2 * gate + o, :].bitcast(FP8X4),
-                        rhs_scale=w_planes[:, 2 * gate + o, :],
-                        start=(o == 0),
-                        stop=(o == 1),
-                    )
-                nc.vector.tensor_tensor(out=dest, in0=acc[:], in1=bias[:, gate, :], op=ADD)
+        def product(engine, t, gate_i, c_head):
+            result = gates.tile([P, UNITS], F32)
+            engine.tensor_tensor(out=result[:], in0=gate_i[:], in1=c_head[:], op=MULT)
+            nc.sync.dma_start(out=out_rows[:, t, :], in_=result[:])
 
-            def product(engine, first, gate_i, c_head):
-                result = gates.tile([P, GROUP, UNITS], F32)
-                engine.tensor_tensor(out=result[:], in0=gate_i[:], in1=c_head[:], op=MULT)
-                nc.sync.dma_start(out=out_rows[:, first : first + GROUP, :], in_=result[:])
+        transpose_round(0)
+        for gate in range(2):
+            acc = psum_mx.tile([P, UNITS], F32)
+            nc.tensor.matmul(out=acc[:], lhsT=ones[:], rhs=bias_rows[:, gate, :], start=True, stop=True)
+            nc.vector.tensor_copy(out=bias[:, gate, :], in_=acc[:])
+        quantise_round(0)
 
-            left_to_vector = []
-            for first in range(0, TILES, GROUP):
-                gate_i = gates.tile([P, GROUP, UNITS], F32)
-                c_head = gates.tile([P, GROUP, UNITS], F32)
-                for g in range(GROUP):
-                    biased_sum(first + g, 0, gate_i[:, g, :])
-                    nc.scalar.activation(out=gate_i[:, g, :], in_=gate_i[:, g, :], func=SIGMOID)
-                    biased_sum(first + g, 1, c_head[:, g, :])
-                if first < TILES - VECTOR_GROUPS * GROUP:
-                    product(nc.gpsimd, first, gate_i, c_head)
+        left_to_vector = []
+        for r in range(ROUNDS):
+            if r + 1 < ROUNDS:
+                transpose_round(r + 1)
+            for j in range(ROUND):
+                t = r * ROUND + j
+                gate_i = gates.tile([P, UNITS], F32)
+                c_head = gates.tile([P, UNITS], F32)
+                biased_sum(t, 0, gate_i[:])
+                nc.scalar.activation(out=gate_i[:], in_=gate_i[:], func=SIGMOID)
+                biased_sum(t, 1, c_head[:])
+                if t < TILES - VECTOR_TILES:
+                    product(nc.gpsimd, t, gate_i, c_head)
                 else:
-                    left_to_vector.append((first, gate_i, c_head))
-            for first, gate_i, c_head in left_to_vector:
-                product(nc.vector, first, gate_i, c_head)
+                    left_to_vector.append((t, gate_i, c_head))
+                if j == QUANTISE_AFTER and r + 1 < ROUNDS:
+                    quantise_round(r + 1)
+        for t, gate_i, c_head in left_to_vector:
+            product(nc.vector, t, gate_i, c_head)

@@ -24,6 +24,7 @@ ROUNDS = TILES // ROUND
 PAIR = 2
 T_BANKS = 4
 MX_BANKS = 4
+LEAD = 3
 QUANTISE_AFTER = 1
 VECTOR_TILES = 2
 
@@ -57,7 +58,7 @@ def tile_lstmcell_pa_t_kernel(
     with ExitStack() as ctx:
         ctx.enter_context(tc.manual_schedule())
         const = ctx.enter_context(tc.tile_pool(name="const", bufs=1))
-        stage = ctx.enter_context(tc.tile_pool(name="stage", bufs=2))
+        stage = ctx.enter_context(tc.tile_pool(name="stage", bufs=3))
         gates = ctx.enter_context(tc.tile_pool(name="gates", bufs=6))
         psum_t = ctx.enter_context(tc.psum_pool(name="psum_t", bufs=T_BANKS))
         psum_mx = ctx.enter_context(tc.psum_pool(name="psum_mx", bufs=MX_BANKS))
@@ -82,11 +83,13 @@ def tile_lstmcell_pa_t_kernel(
             [const.tile([P, ROUND, K], BF16, name="acts_%d_%d" % (r, o)) for o in range(2)] for r in range(ROUNDS)
         ]
 
-        def load_round(r):
+        def load_round(queue, r):
             for o in range(2):
-                nc.sync.dma_start(out=acts[r][o][:], in_=operand_rows[o][:, r * ROUND : (r + 1) * ROUND, :])
+                queue.dma_start(out=acts[r][o][:], in_=operand_rows[o][:, r * ROUND : (r + 1) * ROUND, :])
 
-        load_round(0)
+        load_round(nc.sync, 0)
+        for r in range(1, LEAD):
+            load_round(nc.gpsimd, r)
         for w in range(4):
             scale_rows = weights[w][1].rearrange("g (a r) n -> r (g a) n", r=4)
             for r in range(4):
@@ -97,8 +100,8 @@ def tile_lstmcell_pa_t_kernel(
                 out=w_codes[:, w, :].bitcast(I32),
                 in_=weights[w][0].rearrange("g p n t -> (g p) (n t)").bitcast(I32),
             )
-        for r in range(1, ROUNDS):
-            load_round(r)
+        for r in range(LEAD, ROUNDS):
+            load_round(nc.sync, r)
 
         codes = [const.tile([P, 2 * ROUND * P], U32, name="codes_%d" % r, align_bytes=64) for r in range(ROUNDS)]
         planes = [const.tile([P, 2 * ROUND * P], U8, name="planes_%d" % r, align_bytes=64) for r in range(ROUNDS)]
@@ -152,11 +155,12 @@ def tile_lstmcell_pa_t_kernel(
             nc.tensor.matmul(out=acc[:], lhsT=ones[:], rhs=bias_rows[:, gate, :], start=True, stop=True)
             nc.vector.tensor_copy(out=bias[:, gate, :], in_=acc[:])
         quantise_round(0)
+        for r in range(1, LEAD):
+            transpose_round(r)
+            quantise_round(r)
 
         left_to_vector = []
         for r in range(ROUNDS):
-            if r + 1 < ROUNDS:
-                transpose_round(r + 1)
             for j in range(ROUND):
                 t = r * ROUND + j
                 gate_i = gates.tile([P, UNITS], F32)
@@ -168,7 +172,9 @@ def tile_lstmcell_pa_t_kernel(
                     product(nc.gpsimd, t, gate_i, c_head)
                 else:
                     left_to_vector.append((t, gate_i, c_head))
-                if j == QUANTISE_AFTER and r + 1 < ROUNDS:
-                    quantise_round(r + 1)
+                if j == QUANTISE_AFTER and 1 <= r <= ROUNDS - LEAD:
+                    quantise_round(r + LEAD - 1)
+            if r + LEAD < ROUNDS:
+                transpose_round(r + LEAD)
         for t, gate_i, c_head in left_to_vector:
             product(nc.vector, t, gate_i, c_head)

@@ -26,6 +26,7 @@ T_BANKS = 4
 MX_BANKS = 4
 LEAD = 3
 QUANTISE_AFTER = 1
+SORTED_FROM = 4
 VECTOR_TILES = 2
 
 FLOPS = 4 * 2 * BATCH * K * UNITS
@@ -60,6 +61,7 @@ def tile_lstmcell_pa_t_kernel(
         const = ctx.enter_context(tc.tile_pool(name="const", bufs=1))
         stage = ctx.enter_context(tc.tile_pool(name="stage", bufs=3))
         gates = ctx.enter_context(tc.tile_pool(name="gates", bufs=6))
+        sorting = ctx.enter_context(tc.tile_pool(name="sorting", bufs=2))
         psum_t = ctx.enter_context(tc.psum_pool(name="psum_t", bufs=T_BANKS))
         psum_mx = ctx.enter_context(tc.psum_pool(name="psum_mx", bufs=MX_BANKS))
 
@@ -106,12 +108,21 @@ def tile_lstmcell_pa_t_kernel(
         codes = [const.tile([P, 2 * ROUND * P], U32, name="codes_%d" % r, align_bytes=64) for r in range(ROUNDS)]
         planes = [const.tile([P, 2 * ROUND * P], U8, name="planes_%d" % r, align_bytes=64) for r in range(ROUNDS)]
         grouped_of = [None] * ROUNDS
+        sorted_of = [None] * ROUNDS
+
+        def sort_round(r):
+            sorted_words = sorting.tile([P, ROUND, 2, P], F32)
+            nc.scalar.copy(out=sorted_words[:], in_=acts[r][0][:].bitcast(F32).rearrange("p j (w u) -> p j u w", u=2))
+            sorted_of[r] = sorted_words
 
         def transpose_round(r):
             grouped = stage.tile([P, 2 * ROUND * P * PACK], BF16, align_bytes=64)
             grouped_words = grouped[:].bitcast(F32).rearrange("p (c j b u) -> p c j b u", j=PAIR, b=P, u=2)
             for o in range(2):
-                row_words = acts[r][o][:].bitcast(F32).rearrange("p j (w u) -> p j u w", u=2)
+                if o == 0 and sorted_of[r] is not None:
+                    row_words = sorted_of[r][:]
+                else:
+                    row_words = acts[r][o][:].bitcast(F32).rearrange("p j (w u) -> p j u w", u=2)
                 for pair in range(ROUND // PAIR):
                     bank = psum_t.tile([P, PAIR, 2, P], F32)
                     for j in range(PAIR):
@@ -174,6 +185,8 @@ def tile_lstmcell_pa_t_kernel(
                     left_to_vector.append((t, gate_i, c_head))
                 if j == QUANTISE_AFTER and 1 <= r <= ROUNDS - LEAD:
                     quantise_round(r + LEAD - 1)
+                if j == QUANTISE_AFTER and SORTED_FROM <= r + LEAD + 1 < ROUNDS:
+                    sort_round(r + LEAD + 1)
             if r + LEAD < ROUNDS:
                 transpose_round(r + LEAD)
         for t, gate_i, c_head in left_to_vector:

@@ -25,7 +25,7 @@ PAIR = 2
 T_BANKS = 4
 MX_BANKS = 4
 LEAD = 3
-QUANTISE_AFTER = 1
+QUANTISE_AFTER = 3
 SORTED_FROM = 4
 VECTOR_TILES = 2
 

from contextlib import ExitStack

import concourse.mybir as mybir
from concourse.masks import make_identity

F32 = mybir.dt.float32
BF16 = mybir.dt.bfloat16
I32 = mybir.dt.int32
U32 = mybir.dt.uint32
U8 = mybir.dt.uint8
FP8X4 = mybir.dt.float8_e4m3fn_x4
ADD = mybir.AluOpType.add
MULT = mybir.AluOpType.mult
SIGMOID = mybir.ActivationFunctionType.Sigmoid

P = 128
PACK = 4
BATCH = 4096
K = P * PACK
UNITS = 512
TILES = BATCH // P
ROUND = 4
ROUNDS = TILES // ROUND
PAIR = 2
T_BANKS = 4
MX_BANKS = 4
LEAD = 3
QUANTISE_AFTER = 3
SORTED_FROM = 4
VECTOR_TILES = 2

FLOPS = 4 * 2 * BATCH * K * UNITS


def tile_lstmcell_pa_t_kernel(
    tc,
    incoming,
    h,
    W_i_words,
    W_i_scales,
    b_W_i,
    W_c_words,
    W_c_scales,
    b_W_c,
    U_i_words,
    U_i_scales,
    b_U_i,
    U_c_words,
    U_c_scales,
    b_U_c,
    out,
):
    nc = tc.nc
    operand_rows = [a.rearrange("(p t) k -> p t k", t=TILES) for a in (incoming, h)]
    out_rows = out.rearrange("(p t) n -> p t n", t=TILES)
    weights = [(W_i_words, W_i_scales), (U_i_words, U_i_scales), (W_c_words, W_c_scales), (U_c_words, U_c_scales)]
    biases = [(b_W_i, b_U_i), (b_W_c, b_U_c)]

    with ExitStack() as ctx:
        ctx.enter_context(tc.manual_schedule())
        const = ctx.enter_context(tc.tile_pool(name="const", bufs=1))
        stage = ctx.enter_context(tc.tile_pool(name="stage", bufs=3))
        gates = ctx.enter_context(tc.tile_pool(name="gates", bufs=6))
        sorting = ctx.enter_context(tc.tile_pool(name="sorting", bufs=2))
        psum_t = ctx.enter_context(tc.psum_pool(name="psum_t", bufs=T_BANKS))
        psum_mx = ctx.enter_context(tc.psum_pool(name="psum_mx", bufs=MX_BANKS))

        w_planes = const.tile([P, 4, UNITS], U8, align_bytes=64)
        nc.vector.memset(w_planes[:].rearrange("p w n -> p (w n)").bitcast(I32), 0)
        ident = const.tile([P, P], F32)
        make_identity(nc, ident[:])
        ones = const.tile([P, P], BF16)
        nc.vector.memset(ones[:], 1.0)
        bias_rows = const.tile([P, 2, UNITS], BF16)
        nc.vector.memset(bias_rows[:], 0.0)
        warm = const.tile([P, 1], F32)
        nc.vector.memset(warm[:], 0.0)

        for gate in range(2):
            for row in range(2):
                nc.scalar.dma_start(out=bias_rows[row : row + 1, gate, :], in_=biases[gate][row].unsqueeze(0))
        nc.scalar.activation(out=warm[:], in_=warm[:], func=SIGMOID)

        acts = [
            [const.tile([P, ROUND, K], BF16, name="acts_%d_%d" % (r, o)) for o in range(2)] for r in range(ROUNDS)
        ]

        def load_round(queue, r):
            for o in range(2):
                queue.dma_start(out=acts[r][o][:], in_=operand_rows[o][:, r * ROUND : (r + 1) * ROUND, :])

        load_round(nc.sync, 0)
        for r in range(1, LEAD):
            load_round(nc.gpsimd, r)
        for w in range(4):
            scale_rows = weights[w][1].rearrange("g (a r) n -> r (g a) n", r=4)
            for r in range(4):
                nc.sync.dma_start(out=w_planes[r:P:32, w, :].bitcast(I32), in_=scale_rows[r].bitcast(I32))
        w_codes = const.tile([P, 4, PACK * UNITS], U8, align_bytes=64)
        for w in range(4):
            nc.sync.dma_start(
                out=w_codes[:, w, :].bitcast(I32),
                in_=weights[w][0].rearrange("g p n t -> (g p) (n t)").bitcast(I32),
            )
        for r in range(LEAD, ROUNDS):
            load_round(nc.sync, r)

        codes = [const.tile([P, 2 * ROUND * P], U32, name="codes_%d" % r, align_bytes=64) for r in range(ROUNDS)]
        planes = [const.tile([P, 2 * ROUND * P], U8, name="planes_%d" % r, align_bytes=64) for r in range(ROUNDS)]
        grouped_of = [None] * ROUNDS
        sorted_of = [None] * ROUNDS

        def sort_round(r):
            sorted_words = sorting.tile([P, ROUND, 2, P], F32)
            nc.scalar.copy(out=sorted_words[:], in_=acts[r][0][:].bitcast(F32).rearrange("p j (w u) -> p j u w", u=2))
            sorted_of[r] = sorted_words

        def transpose_round(r):
            grouped = stage.tile([P, 2 * ROUND * P * PACK], BF16, align_bytes=64)
            grouped_words = grouped[:].bitcast(F32).rearrange("p (c j b u) -> p c j b u", j=PAIR, b=P, u=2)
            for o in range(2):
                if o == 0 and sorted_of[r] is not None:
                    row_words = sorted_of[r][:]
                else:
                    row_words = acts[r][o][:].bitcast(F32).rearrange("p j (w u) -> p j u w", u=2)
                for pair in range(ROUND // PAIR):
                    bank = psum_t.tile([P, PAIR, 2, P], F32)
                    for j in range(PAIR):
                        for u in range(2):
                            nc.tensor.transpose(bank[:, j, u, :], row_words[:, pair * PAIR + j, u, :], ident[:])
                    nc.scalar.copy(
                        out=grouped_words[:, o * (ROUND // PAIR) + pair],
                        in_=bank[:].rearrange("p j u b -> p j b u"),
                    )
            grouped_of[r] = grouped

        def quantise_round(r):
            nc.vector.quantize_mx(out=codes[r][:].bitcast(FP8X4), scales=planes[r][:], in_=grouped_of[r][:])

        bias = const.tile([P, 2, UNITS], F32)

        def biased_sum(t, gate, dest):
            r, j = divmod(t, ROUND)
            acc = psum_mx.tile([P, UNITS], F32)
            for o in range(2):
                cols = slice((o * ROUND + j) * P, (o * ROUND + j + 1) * P)
                nc.tensor.matmul_mx(
                    out=acc[:],
                    lhsT=codes[r][:, cols].bitcast(FP8X4),
                    lhsT_scale=planes[r][:, cols],
                    rhs=w_codes[:, 2 * gate + o, :].bitcast(FP8X4),
                    rhs_scale=w_planes[:, 2 * gate + o, :],
                    start=(o == 0),
                    stop=(o == 1),
                )
            nc.vector.tensor_tensor(out=dest, in0=acc[:], in1=bias[:, gate, :], op=ADD)

        def product(engine, t, gate_i, c_head):
            result = gates.tile([P, UNITS], F32)
            engine.tensor_tensor(out=result[:], in0=gate_i[:], in1=c_head[:], op=MULT)
            nc.sync.dma_start(out=out_rows[:, t, :], in_=result[:])

        transpose_round(0)
        for gate in range(2):
            acc = psum_mx.tile([P, UNITS], F32)
            nc.tensor.matmul(out=acc[:], lhsT=ones[:], rhs=bias_rows[:, gate, :], start=True, stop=True)
            nc.vector.tensor_copy(out=bias[:, gate, :], in_=acc[:])
        quantise_round(0)
        for r in range(1, LEAD):
            transpose_round(r)
            quantise_round(r)

        left_to_vector = []
        for r in range(ROUNDS):
            for j in range(ROUND):
                t = r * ROUND + j
                gate_i = gates.tile([P, UNITS], F32)
                c_head = gates.tile([P, UNITS], F32)
                biased_sum(t, 0, gate_i[:])
                nc.scalar.activation(out=gate_i[:], in_=gate_i[:], func=SIGMOID)
                biased_sum(t, 1, c_head[:])
                if t < TILES - VECTOR_TILES:
                    product(nc.gpsimd, t, gate_i, c_head)
                else:
                    left_to_vector.append((t, gate_i, c_head))
                if j == QUANTISE_AFTER and 1 <= r <= ROUNDS - LEAD:
                    quantise_round(r + LEAD - 1)
                if j == QUANTISE_AFTER and SORTED_FROM <= r + LEAD + 1 < ROUNDS:
                    sort_round(r + LEAD + 1)
            if r + LEAD < ROUNDS:
                transpose_round(r + LEAD)
        for t, gate_i, c_head in left_to_vector:
            product(nc.vector, t, gate_i, c_head)
